import numpy as np
import ml_dtypes


def mxq(x, axis, fmt="e4m3"):
    dtype, down = {"e4m3": (ml_dtypes.float8_e4m3fn, 7), "e5m2": (ml_dtypes.float8_e5m2, 14)}[fmt]
    v = np.moveaxis(np.asarray(x, np.float32).astype(ml_dtypes.bfloat16).astype(np.float64), axis, -1)
    blocks = v.reshape(v.shape[:-1] + (-1, 32))
    amax = np.abs(blocks).max(-1, keepdims=True)
    byte = np.maximum(np.where(amax > 0, np.frexp(amax)[1] - 1 + 127, 0) - down, 1)
    scale = np.exp2(byte - 127.0)
    codes = (blocks / scale).astype(np.float32).astype(dtype).astype(np.float64)
    return np.moveaxis((codes * scale).reshape(v.shape), -1, axis)


WIDE = False


def mx_kscale(k):
    if not WIDE:
        return np.ones(k)
    levels = np.array([20, -20, 10, -10, 0])
    a = np.random.permutation(np.resize(levels, k // 512 * 4)).reshape(k // 512, 4)
    idx = np.arange(k)
    return np.exp2(a[idx // 512, idx % 128 // 32])


BF16 = ml_dtypes.bfloat16


def bf(x):
    return np.asarray(x, np.float32).astype(BF16)


def f64(x):
    return np.asarray(x).astype(np.float64)


B, IN_F, OUT_F = 4096, 1024, 512
EPS = 1e-5


def setup_inputs():
    u = mx_kscale(OUT_F)
    scale = 1.0 / np.sqrt(IN_F)
    x = np.random.standard_normal((B, IN_F))
    y = np.random.standard_normal((B, OUT_F))
    weight = np.random.uniform(-scale, scale, (OUT_F, IN_F)) / u[:, None]
    bias = np.random.uniform(-0.5, 0.5, OUT_F)
    running_mean = np.random.standard_normal(OUT_F) * 0.3
    running_var = np.random.uniform(0.5, 1.5, OUT_F)
    norm_weight = 1.0 + 0.1 * np.random.standard_normal(OUT_F)
    norm_bias = np.random.standard_normal(OUT_F) * 0.3
    g = np.random.standard_normal((B, OUT_F)) * np.exp2(np.random.randint(-12, 1, (B, 1))) * 8.0 * u[None, :]
    return {"x": bf(x), "y": bf(y), "weight": bf(weight), "bias": bf(bias),
            "running_mean": bf(running_mean), "running_var": bf(running_var),
            "norm_weight": bf(norm_weight), "norm_bias": bf(norm_bias),
            "grad_out": bf(g)}


def reference(x, y, weight, bias, running_mean, running_var, norm_weight, norm_bias, grad_out):
    c = f64(norm_weight) / np.sqrt(f64(running_var) + EPS)
    t = f64(grad_out) * f64(y) * c[None, :]
    return mxq(t, 1, "e5m2") @ mxq(f64(weight), 0, "e4m3")

@@ -1,0 +1,210 @@
+from contextlib import ExitStack
+
+import concourse.mybir as mybir
+from concourse.masks import make_identity
+
+F32 = mybir.dt.float32
+BF16 = mybir.dt.bfloat16
+U32 = mybir.dt.uint32
+U8 = mybir.dt.uint8
+E4 = mybir.dt.float8_e4m3fn_x4
+E5 = mybir.dt.float8_e5m2_x4
+MULT = mybir.AluOpType.mult
+ADD = mybir.AluOpType.add
+
+B, IN_F, OUT_F = 4096, 1024, 512
+EPS = 1e-5
+P = 128
+PACK = 4
+NT = B // P
+NH = 512
+GT = 2
+NG = NT // GT
+
+FLOPS = 2 * B * IN_F * OUT_F
+BYTES = 2 * B * OUT_F * 2 + OUT_F * IN_F * 2 + 2 * OUT_F * 2 + B * IN_F * 4
+
+MANUAL = True
+CHUNKS = ((0, 2), (2, 2), (4, 4), (8, 8), (16, 8), (24, 8))
+G_MULT = ()
+G_LEAD = 2
+OUT_BUFS = 8
+
+
+def tile_modelnew_t_kernel(
+    tc, x, y, weight, bias, running_mean, running_var, norm_weight, norm_bias, grad_out, out
+):
+    nc = tc.nc
+    g_v = grad_out.rearrange("(p j) k -> p j k", j=NT)
+    y_v = y.rearrange("(p j) k -> p j k", j=NT)
+    o_v = out.rearrange("(p j) n -> p j n", j=NT)
+    w_v = weight.rearrange("(t p) n -> p t n", p=P)
+
+    with ExitStack() as ctx:
+        keep = ctx.enter_context(tc.tile_pool(name="keep", bufs=1))
+        prod = ctx.enter_context(tc.tile_pool(name="prod", bufs=6))
+        grps = ctx.enter_context(tc.tile_pool(name="grps", bufs=3))
+        code = ctx.enter_context(tc.tile_pool(name="code", bufs=3))
+        outs = ctx.enter_context(tc.tile_pool(name="outs", bufs=OUT_BUFS))
+        ps_t = ctx.enter_context(tc.psum_pool(name="ps_t", bufs=4))
+        ps_m = ctx.enter_context(tc.psum_pool(name="ps_m", bufs=4))
+        if MANUAL:
+            ctx.enter_context(tc.manual_schedule())
+
+        vec = keep.tile([P, P], BF16, name="vec")
+        nc.vector.memset(vec[:], 0.0)
+        nc.scalar.dma_start(out=vec[0:4, :], in_=running_var.rearrange("(t p) -> t p", p=P))
+        nc.scalar.dma_start(out=vec[4:8, :], in_=norm_weight.rearrange("(t p) -> t p", p=P))
+        one = keep.tile([P, 1], F32, name="one")
+        nc.vector.memset(one[:], 1.0)
+        warm = keep.tile([P, 1], F32, name="warm")
+        nc.scalar.sqrt(out=warm[:], in_=one[:])
+
+        g_sb = []
+        y_sb = []
+        w_sb = keep.tile([P, PACK, IN_F], BF16, name="w_sb")
+        for c, (j0, nj) in enumerate(CHUNKS):
+            gt = keep.tile([P, nj, OUT_F], BF16, name="g%d" % c)
+            yt = keep.tile([P, nj, OUT_F], BF16, name="y%d" % c)
+            nc.sync.dma_start(out=gt[:], in_=g_v[:, j0 : j0 + nj, :])
+            nc.sync.dma_start(out=yt[:], in_=y_v[:, j0 : j0 + nj, :])
+            g_sb.append(gt)
+            y_sb.append(yt)
+            if c == 0:
+                nc.sync.dma_start(out=w_sb[:], in_=w_v)
+
+        ident_b = keep.tile([P, P], BF16, name="ident_b")
+        make_identity(nc, ident_b[:])
+        ident = keep.tile([P, P], F32, name="ident")
+        make_identity(nc, ident[:])
+
+        def where(g):
+            j = g * GT
+            for c, (j0, nj) in enumerate(CHUNKS):
+                if j0 <= j < j0 + nj:
+                    return g_sb[c], y_sb[c], j - j0
+            raise ValueError("no chunk")
+
+        prods = {}
+        banks = {}
+        words = {}
+
+        def product(g):
+            gt, yt, j = where(g)
+            pt = prod.tile([P, GT, OUT_F], F32, name="pt")
+            eng = nc.gpsimd if g in G_MULT else nc.vector
+            eng.tensor_tensor(out=pt[:], in0=gt[:, j : j + GT, :], in1=yt[:, j : j + GT, :], op=MULT)
+            prods[g] = pt
+
+        def flip(g):
+            pt = prods[g]
+            got = []
+            for i in range(GT):
+                tp = ps_t.tile([P, PACK, P], F32, name="tp")
+                for t in range(PACK):
+                    nc.tensor.transpose(tp[:, t, :], pt[:, i, t * P : (t + 1) * P], ident[:])
+                got.append(tp)
+            banks[g] = got
+
+        def scale_quantise(g):
+            gr = grps.tile([P, GT, P, PACK], BF16, name="gr", align_bytes=64)
+            cd = code.tile([P, GT * P], U32, name="cd", align_bytes=64)
+            sc = code.tile([P, GT * P], U8, name="sc", align_bytes=64)
+            for i in range(GT):
+                nc.vector.tensor_tensor(
+                    out=gr[:, i, :, :],
+                    in0=banks[g][i][:].rearrange("p t m -> p m t"),
+                    in1=c_bc,
+                    op=MULT,
+                )
+            for i in range(GT):
+                nc.vector.quantize_mx(
+                    out=cd[:, i * P : (i + 1) * P].bitcast(E5),
+                    scales=sc[:, i * P : (i + 1) * P],
+                    in_=gr[:, i, :, :].rearrange("p m t -> p (m t)"),
+                )
+            words[g] = (cd, sc)
+
+        def multiply_store(g):
+            cd, sc = words[g]
+            ot = outs.tile([P, GT, IN_F], F32, name="ot")
+            for h in range(2):
+                for i in range(GT):
+                    acc = ps_m.tile([P, NH], F32, name="acc")
+                    nc.tensor.matmul_mx(
+                        out=acc[:],
+                        lhsT=cd[:, i * P : (i + 1) * P].bitcast(E5),
+                        lhsT_scale=sc[:, i * P : (i + 1) * P],
+                        rhs=w_cd[h][:].bitcast(E4),
+                        rhs_scale=w_sc[h][:],
+                        start=True,
+                        stop=True,
+                    )
+                    nc.scalar.copy(out=ot[:, i, h * NH : (h + 1) * NH], in_=acc[:])
+            nc.sync.dma_start(out=o_v[:, g * GT : (g + 1) * GT, :], in_=ot[:])
+
+        vT = ps_t.tile([P, P], BF16, name="vT", tag="tp")
+        nc.tensor.transpose(vT[:], vec[:], ident_b[:])
+        var = keep.tile([P, PACK], F32, name="var")
+        nc.vector.tensor_scalar_add(out=var[:], in0=vT[:, 0:PACK], scalar1=EPS)
+        sd = keep.tile([P, PACK], F32, name="sd")
+        nc.scalar.sqrt(out=sd[:], in_=var[:])
+
+        issued = set()
+
+        def issue_product(g):
+            if 0 <= g < NG and g not in issued:
+                issued.add(g)
+                product(g)
+
+        issue_product(0)
+
+        r0 = keep.tile([P, PACK], F32, name="r0")
+        nc.vector.reciprocal(out=r0[:], in_=sd[:])
+        hn = keep.tile([P, PACK], F32, name="hn")
+        nc.vector.scalar_tensor_tensor(out=hn[:], in0=r0[:], scalar=-0.5, in1=r0[:], op0=MULT, op1=MULT)
+        rn = keep.tile([P, PACK], F32, name="rn")
+        nc.vector.tensor_tensor(out=rn[:], in0=vT[:, PACK : 2 * PACK], in1=r0[:], op=MULT)
+        ev = keep.tile([P, PACK], F32, name="ev")
+        nc.vector.tensor_tensor(out=ev[:], in0=hn[:], in1=var[:], op=MULT)
+        c_sb = keep.tile([P, PACK], F32, name="c_sb")
+        nc.vector.scalar_tensor_tensor(out=c_sb[:], in0=ev[:], scalar=1.5, in1=rn[:], op0=ADD, op1=MULT)
+        c_bc = c_sb[:].unsqueeze(1).to_broadcast([P, P, PACK])
+
+        w_gr = []
+        w_cd = []
+        w_sc = []
+        for h in range(2):
+            wg = keep.tile([P, NH, PACK], BF16, name="wg%d" % h, align_bytes=64)
+            src = w_sb[:, :, h * NH : (h + 1) * NH].rearrange("p t (c i) -> p c t i", i=4)
+            dst = wg[:].rearrange("p (c i) t -> p c t i", i=4)
+            if h == 0:
+                nc.vector.tensor_copy(out=dst, in_=src)
+            else:
+                nc.scalar.copy(out=dst, in_=src)
+            w_gr.append(wg)
+            w_cd.append(keep.tile([P, NH], U32, name="wc%d" % h, align_bytes=64))
+            w_sc.append(keep.tile([P, NH], U8, name="ws%d" % h, align_bytes=64))
+
+        flip(0)
+        for g in range(NG):
+            if g in G_MULT and g <= 2 + G_LEAD:
+                issue_product(g)
+        issue_product(1)
+        scale_quantise(0)
+        for h in range(2):
+            nc.vector.quantize_mx(
+                out=w_cd[h][:].bitcast(E4),
+                scales=w_sc[h][:],
+                in_=w_gr[h][:].rearrange("p n t -> p (n t)"),
+            )
+
+        for g in range(NG):
+            if g + 1 < NG:
+                flip(g + 1)
+            if (g + 2 + G_LEAD) in G_MULT:
+                issue_product(g + 2 + G_LEAD)
+            issue_product(g + 2)
+            multiply_store(g)
+            if g + 1 < NG:
+                scale_quantise(g + 1)

@@ -24,9 +24,8 @@ NG = NT // GT
 FLOPS = 2 * B * IN_F * OUT_F
 BYTES = 2 * B * OUT_F * 2 + OUT_F * IN_F * 2 + 2 * OUT_F * 2 + B * IN_F * 4
 
-MANUAL = True
 CHUNKS = ((0, 2), (2, 2), (4, 4), (8, 8), (16, 8), (24, 8))
-G_MULT = ()
+G_SPLIT = True
 G_LEAD = 2
 OUT_BUFS = 8
 
@@ -42,19 +41,16 @@ def tile_modelnew_t_kernel(
 
     with ExitStack() as ctx:
         keep = ctx.enter_context(tc.tile_pool(name="keep", bufs=1))
-        prod = ctx.enter_context(tc.tile_pool(name="prod", bufs=6))
+        prod = ctx.enter_context(tc.tile_pool(name="prod", bufs=4))
         grps = ctx.enter_context(tc.tile_pool(name="grps", bufs=3))
         code = ctx.enter_context(tc.tile_pool(name="code", bufs=3))
         outs = ctx.enter_context(tc.tile_pool(name="outs", bufs=OUT_BUFS))
         ps_t = ctx.enter_context(tc.psum_pool(name="ps_t", bufs=4))
         ps_m = ctx.enter_context(tc.psum_pool(name="ps_m", bufs=4))
-        if MANUAL:
-            ctx.enter_context(tc.manual_schedule())
+        ctx.enter_context(tc.manual_schedule())
 
         vec = keep.tile([P, P], BF16, name="vec")
         nc.vector.memset(vec[:], 0.0)
-        nc.scalar.dma_start(out=vec[0:4, :], in_=running_var.rearrange("(t p) -> t p", p=P))
-        nc.scalar.dma_start(out=vec[4:8, :], in_=norm_weight.rearrange("(t p) -> t p", p=P))
         one = keep.tile([P, 1], F32, name="one")
         nc.vector.memset(one[:], 1.0)
         warm = keep.tile([P, 1], F32, name="warm")
@@ -71,6 +67,8 @@ def tile_modelnew_t_kernel(
             g_sb.append(gt)
             y_sb.append(yt)
             if c == 0:
+                nc.sync.dma_start(out=vec[0:4, :], in_=running_var.rearrange("(t p) -> t p", p=P))
+                nc.sync.dma_start(out=vec[4:8, :], in_=norm_weight.rearrange("(t p) -> t p", p=P))
                 nc.sync.dma_start(out=w_sb[:], in_=w_v)
 
         ident_b = keep.tile([P, P], BF16, name="ident_b")
@@ -87,29 +85,45 @@ def tile_modelnew_t_kernel(
 
         prods = {}
         banks = {}
+        grouped = {}
         words = {}
 
-        def product(g):
+        def product(g, i):
+            if not 0 <= g < NG or (g, i) in prods:
+                return
             gt, yt, j = where(g)
-            pt = prod.tile([P, GT, OUT_F], F32, name="pt")
-            eng = nc.gpsimd if g in G_MULT else nc.vector
-            eng.tensor_tensor(out=pt[:], in0=gt[:, j : j + GT, :], in1=yt[:, j : j + GT, :], op=MULT)
-            prods[g] = pt
+            if i is None:
+                pt = prod.tile([P, GT, OUT_F], F32, name="pt")
+                nc.vector.tensor_tensor(out=pt[:], in0=gt[:, j : j + GT, :], in1=yt[:, j : j + GT, :], op=MULT)
+                prods[(g, None)] = pt
+                prods[(g, 0)] = pt[:, 0, :]
+                prods[(g, 1)] = pt[:, 1, :]
+                return
+            pt = prod.tile([P, OUT_F], F32, name="pt%d" % i)
+            eng = nc.gpsimd if i == 1 else nc.vector
+            eng.tensor_tensor(out=pt[:], in0=gt[:, j + i, :], in1=yt[:, j + i, :], op=MULT)
+            prods[(g, i)] = pt[:]
+
+        def products(g):
+            if G_SPLIT:
+                for ahead in range(g + G_LEAD + 1):
+                    product(ahead, 1)
+                product(g, 0)
+            else:
+                product(g, None)
 
         def flip(g):
-            pt = prods[g]
             got = []
             for i in range(GT):
+                pt = prods[(g, i)]
                 tp = ps_t.tile([P, PACK, P], F32, name="tp")
                 for t in range(PACK):
-                    nc.tensor.transpose(tp[:, t, :], pt[:, i, t * P : (t + 1) * P], ident[:])
+                    nc.tensor.transpose(tp[:, t, :], pt[:, t * P : (t + 1) * P], ident[:])
                 got.append(tp)
             banks[g] = got
 
-        def scale_quantise(g):
+        def scale(g):
             gr = grps.tile([P, GT, P, PACK], BF16, name="gr", align_bytes=64)
-            cd = code.tile([P, GT * P], U32, name="cd", align_bytes=64)
-            sc = code.tile([P, GT * P], U8, name="sc", align_bytes=64)
             for i in range(GT):
                 nc.vector.tensor_tensor(
                     out=gr[:, i, :, :],
@@ -117,6 +131,12 @@ def tile_modelnew_t_kernel(
                     in1=c_bc,
                     op=MULT,
                 )
+            grouped[g] = gr
+
+        def quantise(g):
+            gr = grouped[g]
+            cd = code.tile([P, GT * P], U32, name="cd", align_bytes=64)
+            sc = code.tile([P, GT * P], U8, name="sc", align_bytes=64)
             for i in range(GT):
                 nc.vector.quantize_mx(
                     out=cd[:, i * P : (i + 1) * P].bitcast(E5),
@@ -127,7 +147,13 @@ def tile_modelnew_t_kernel(
 
         def multiply_store(g):
             cd, sc = words[g]
-            ot = outs.tile([P, GT, IN_F], F32, name="ot")
+            last = g == NG - 1
+            if last:
+                ots = [outs.tile([P, IN_F], F32, name="ol%d" % i, bufs=1) for i in range(GT)]
+                dsts = [ots[i][:] for i in range(GT)]
+            else:
+                ot = outs.tile([P, GT, IN_F], F32, name="ot")
+                dsts = [ot[:, i, :] for i in range(GT)]
             for h in range(2):
                 for i in range(GT):
                     acc = ps_m.tile([P, NH], F32, name="acc")
@@ -140,8 +166,17 @@ def tile_modelnew_t_kernel(
                         start=True,
                         stop=True,
                     )
-                    nc.scalar.copy(out=ot[:, i, h * NH : (h + 1) * NH], in_=acc[:])
-            nc.sync.dma_start(out=o_v[:, g * GT : (g + 1) * GT, :], in_=ot[:])
+                    if last and i == 1:
+                        nc.vector.tensor_copy(out=dsts[i][:, h * NH : (h + 1) * NH], in_=acc[:])
+                    else:
+                        nc.scalar.copy(out=dsts[i][:, h * NH : (h + 1) * NH], in_=acc[:])
+            if last:
+                for i in range(GT):
+                    nc.sync.dma_start(out=o_v[:, g * GT + i, :], in_=dsts[i])
+            else:
+                nc.sync.dma_start(out=o_v[:, g * GT : (g + 1) * GT, :], in_=ot[:])
+
+        products(0)
 
         vT = ps_t.tile([P, P], BF16, name="vT", tag="tp")
         nc.tensor.transpose(vT[:], vec[:], ident_b[:])
@@ -149,16 +184,7 @@ def tile_modelnew_t_kernel(
         nc.vector.tensor_scalar_add(out=var[:], in0=vT[:, 0:PACK], scalar1=EPS)
         sd = keep.tile([P, PACK], F32, name="sd")
         nc.scalar.sqrt(out=sd[:], in_=var[:])
-
-        issued = set()
-
-        def issue_product(g):
-            if 0 <= g < NG and g not in issued:
-                issued.add(g)
-                product(g)
-
-        issue_product(0)
-
+        flip(0)
         r0 = keep.tile([P, PACK], F32, name="r0")
         nc.vector.reciprocal(out=r0[:], in_=sd[:])
         hn = keep.tile([P, PACK], F32, name="hn")
@@ -170,6 +196,8 @@ def tile_modelnew_t_kernel(
         c_sb = keep.tile([P, PACK], F32, name="c_sb")
         nc.vector.scalar_tensor_tensor(out=c_sb[:], in0=ev[:], scalar=1.5, in1=rn[:], op0=ADD, op1=MULT)
         c_bc = c_sb[:].unsqueeze(1).to_broadcast([P, P, PACK])
+
+        scale(0)
 
         w_gr = []
         w_cd = []
@@ -186,25 +214,28 @@ def tile_modelnew_t_kernel(
             w_cd.append(keep.tile([P, NH], U32, name="wc%d" % h, align_bytes=64))
             w_sc.append(keep.tile([P, NH], U8, name="ws%d" % h, align_bytes=64))
 
-        flip(0)
-        for g in range(NG):
-            if g in G_MULT and g <= 2 + G_LEAD:
-                issue_product(g)
-        issue_product(1)
-        scale_quantise(0)
-        for h in range(2):
+        def quantise_weight(h):
             nc.vector.quantize_mx(
                 out=w_cd[h][:].bitcast(E4),
                 scales=w_sc[h][:],
                 in_=w_gr[h][:].rearrange("p n t -> p (n t)"),
             )
 
+        quantise(0)
+        quantise_weight(0)
+        quantise_weight(1)
+        products(1)
+
         for g in range(NG):
-            if g + 1 < NG:
+            if g == 0:
+                multiply_store(g)
                 flip(g + 1)
-            if (g + 2 + G_LEAD) in G_MULT:
-                issue_product(g + 2 + G_LEAD)
-            issue_product(g + 2)
-            multiply_store(g)
+                products(g + 2)
+            else:
+                if g + 1 < NG:
+                    flip(g + 1)
+                products(g + 2)
+                multiply_store(g)
             if g + 1 < NG:
-                scale_quantise(g + 1)
+                scale(g + 1)
+                quantise(g + 1)

@@ -24,10 +24,11 @@ NG = NT // GT
 FLOPS = 2 * B * IN_F * OUT_F
 BYTES = 2 * B * OUT_F * 2 + OUT_F * IN_F * 2 + 2 * OUT_F * 2 + B * IN_F * 4
 
-CHUNKS = ((0, 2), (2, 2), (4, 4), (8, 8), (16, 8), (24, 8))
+CHUNKS = ((0, 4), (4, 4), (8, 8), (16, 16))
+STORES = (2, 2, 2, 2, 2, 2, 2, 2)
 G_SPLIT = True
 G_LEAD = 2
-OUT_BUFS = 8
+OUT_BUFS = 6
 
 
 def tile_modelnew_t_kernel(
@@ -147,13 +148,10 @@ def tile_modelnew_t_kernel(
 
         def multiply_store(g):
             cd, sc = words[g]
-            last = g == NG - 1
-            if last:
-                ots = [outs.tile([P, IN_F], F32, name="ol%d" % i, bufs=1) for i in range(GT)]
-                dsts = [ots[i][:] for i in range(GT)]
-            else:
-                ot = outs.tile([P, GT, IN_F], F32, name="ot")
-                dsts = [ot[:, i, :] for i in range(GT)]
+            first, count = store_of[g]
+            if g == first:
+                held[first] = outs.tile([P, count * GT, IN_F], F32, name="ot%d" % count)
+            ot = held[first]
             for h in range(2):
                 for i in range(GT):
                     acc = ps_m.tile([P, NH], F32, name="acc")
@@ -166,15 +164,18 @@ def tile_modelnew_t_kernel(
                         start=True,
                         stop=True,
                     )
-                    if last and i == 1:
-                        nc.vector.tensor_copy(out=dsts[i][:, h * NH : (h + 1) * NH], in_=acc[:])
-                    else:
-                        nc.scalar.copy(out=dsts[i][:, h * NH : (h + 1) * NH], in_=acc[:])
-            if last:
-                for i in range(GT):
-                    nc.sync.dma_start(out=o_v[:, g * GT + i, :], in_=dsts[i])
-            else:
-                nc.sync.dma_start(out=o_v[:, g * GT : (g + 1) * GT, :], in_=ot[:])
+                    nc.scalar.copy(out=ot[:, (g - first) * GT + i, h * NH : (h + 1) * NH], in_=acc[:])
+            if g == first + count - 1:
+                nc.sync.dma_start(out=o_v[:, first * GT : (first + count) * GT, :], in_=ot[:])
+
+        store_of = {}
+        held = {}
+        first_group = 0
+        for count in STORES:
+            for g in range(first_group, first_group + count):
+                store_of[g] = (first_group, count)
+            first_group += count
+        assert first_group == NG
 
         products(0)
 

@@ -25,10 +25,11 @@ FLOPS = 2 * B * IN_F * OUT_F
 BYTES = 2 * B * OUT_F * 2 + OUT_F * IN_F * 2 + 2 * OUT_F * 2 + B * IN_F * 4
 
 CHUNKS = ((0, 4), (4, 4), (8, 8), (16, 16))
-STORES = (2, 2, 2, 2, 2, 2, 2, 2)
+STORES = (2, 2, 2, 2, 2, 2, 2, 1, 1)
+V_HELPS_FROM = 13
 G_SPLIT = True
 G_LEAD = 2
-OUT_BUFS = 6
+OUT_BUFS = 5
 
 
 def tile_modelnew_t_kernel(
@@ -150,8 +151,11 @@ def tile_modelnew_t_kernel(
             cd, sc = words[g]
             first, count = store_of[g]
             if g == first:
-                held[first] = outs.tile([P, count * GT, IN_F], F32, name="ot%d" % count)
+                held[first] = outs.tile(
+                    [P, count * GT, IN_F], F32, name="ot%d" % count, bufs=(OUT_BUFS if count == 2 else 2)
+                )
             ot = held[first]
+            late[g] = []
             for h in range(2):
                 for i in range(GT):
                     acc = ps_m.tile([P, NH], F32, name="acc")
@@ -164,12 +168,22 @@ def tile_modelnew_t_kernel(
                         start=True,
                         stop=True,
                     )
-                    nc.scalar.copy(out=ot[:, (g - first) * GT + i, h * NH : (h + 1) * NH], in_=acc[:])
+                    dst = ot[:, (g - first) * GT + i, h * NH : (h + 1) * NH]
+                    if g >= V_HELPS_FROM and i == 1:
+                        late[g].append((dst, acc))
+                    else:
+                        nc.scalar.copy(out=dst, in_=acc[:])
+
+        def finish(g):
+            first, count = store_of[g]
+            for dst, acc in late[g]:
+                nc.vector.tensor_copy(out=dst, in_=acc[:])
             if g == first + count - 1:
-                nc.sync.dma_start(out=o_v[:, first * GT : (first + count) * GT, :], in_=ot[:])
+                nc.sync.dma_start(out=o_v[:, first * GT : (first + count) * GT, :], in_=held[first][:])
 
         store_of = {}
         held = {}
+        late = {}
         first_group = 0
         for count in STORES:
             for g in range(first_group, first_group + count):
@@ -240,3 +254,4 @@ def tile_modelnew_t_kernel(
             if g + 1 < NG:
                 scale(g + 1)
                 quantise(g + 1)
+            finish(g)

@@ -25,11 +25,10 @@ FLOPS = 2 * B * IN_F * OUT_F
 BYTES = 2 * B * OUT_F * 2 + OUT_F * IN_F * 2 + 2 * OUT_F * 2 + B * IN_F * 4
 
 CHUNKS = ((0, 4), (4, 4), (8, 8), (16, 16))
-STORES = (2, 2, 2, 2, 2, 2, 2, 1, 1)
-V_HELPS_FROM = 13
-G_SPLIT = True
+STORES = (2, 2, 2, 2, 2, 2, 2, 2)
+G_SPLIT = False
 G_LEAD = 2
-OUT_BUFS = 5
+OUT_BUFS = 6
 
 
 def tile_modelnew_t_kernel(
@@ -151,11 +150,8 @@ def tile_modelnew_t_kernel(
             cd, sc = words[g]
             first, count = store_of[g]
             if g == first:
-                held[first] = outs.tile(
-                    [P, count * GT, IN_F], F32, name="ot%d" % count, bufs=(OUT_BUFS if count == 2 else 2)
-                )
+                held[first] = outs.tile([P, count * GT, IN_F], F32, name="ot%d" % count)
             ot = held[first]
-            late[g] = []
             for h in range(2):
                 for i in range(GT):
                     acc = ps_m.tile([P, NH], F32, name="acc")
@@ -168,22 +164,12 @@ def tile_modelnew_t_kernel(
                         start=True,
                         stop=True,
                     )
-                    dst = ot[:, (g - first) * GT + i, h * NH : (h + 1) * NH]
-                    if g >= V_HELPS_FROM and i == 1:
-                        late[g].append((dst, acc))
-                    else:
-                        nc.scalar.copy(out=dst, in_=acc[:])
-
-        def finish(g):
-            first, count = store_of[g]
-            for dst, acc in late[g]:
-                nc.vector.tensor_copy(out=dst, in_=acc[:])
+                    nc.scalar.copy(out=ot[:, (g - first) * GT + i, h * NH : (h + 1) * NH], in_=acc[:])
             if g == first + count - 1:
-                nc.sync.dma_start(out=o_v[:, first * GT : (first + count) * GT, :], in_=held[first][:])
+                nc.sync.dma_start(out=o_v[:, first * GT : (first + count) * GT, :], in_=ot[:])
 
         store_of = {}
         held = {}
-        late = {}
         first_group = 0
         for count in STORES:
             for g in range(first_group, first_group + count):
@@ -254,4 +240,3 @@ def tile_modelnew_t_kernel(
             if g + 1 < NG:
                 scale(g + 1)
                 quantise(g + 1)
-            finish(g)

@@ -26,7 +26,7 @@ BYTES = 2 * B * OUT_F * 2 + OUT_F * IN_F * 2 + 2 * OUT_F * 2 + B * IN_F * 4
 
 CHUNKS = ((0, 4), (4, 4), (8, 8), (16, 16))
 STORES = (2, 2, 2, 2, 2, 2, 2, 2)
-G_SPLIT = False
+G_SPLIT = True
 G_LEAD = 2
 OUT_BUFS = 6
 
@@ -48,7 +48,6 @@ def tile_modelnew_t_kernel(
         outs = ctx.enter_context(tc.tile_pool(name="outs", bufs=OUT_BUFS))
         ps_t = ctx.enter_context(tc.psum_pool(name="ps_t", bufs=4))
         ps_m = ctx.enter_context(tc.psum_pool(name="ps_m", bufs=4))
-        ctx.enter_context(tc.manual_schedule())
 
         vec = keep.tile([P, P], BF16, name="vec")
         nc.vector.memset(vec[:], 0.0)

from contextlib import ExitStack

import concourse.mybir as mybir
from concourse.masks import make_identity

F32 = mybir.dt.float32
BF16 = mybir.dt.bfloat16
U32 = mybir.dt.uint32
U8 = mybir.dt.uint8
E4 = mybir.dt.float8_e4m3fn_x4
E5 = mybir.dt.float8_e5m2_x4
MULT = mybir.AluOpType.mult
ADD = mybir.AluOpType.add

B, IN_F, OUT_F = 4096, 1024, 512
EPS = 1e-5
P = 128
PACK = 4
NT = B // P
NH = 512
GT = 2
NG = NT // GT

FLOPS = 2 * B * IN_F * OUT_F
BYTES = 2 * B * OUT_F * 2 + OUT_F * IN_F * 2 + 2 * OUT_F * 2 + B * IN_F * 4

CHUNKS = ((0, 4), (4, 4), (8, 8), (16, 16))
STORES = (2, 2, 2, 2, 2, 2, 2, 2)
G_SPLIT = True
G_LEAD = 2
OUT_BUFS = 6


def tile_modelnew_t_kernel(
    tc, x, y, weight, bias, running_mean, running_var, norm_weight, norm_bias, grad_out, out
):
    nc = tc.nc
    g_v = grad_out.rearrange("(p j) k -> p j k", j=NT)
    y_v = y.rearrange("(p j) k -> p j k", j=NT)
    o_v = out.rearrange("(p j) n -> p j n", j=NT)
    w_v = weight.rearrange("(t p) n -> p t n", p=P)

    with ExitStack() as ctx:
        keep = ctx.enter_context(tc.tile_pool(name="keep", bufs=1))
        prod = ctx.enter_context(tc.tile_pool(name="prod", bufs=4))
        grps = ctx.enter_context(tc.tile_pool(name="grps", bufs=3))
        code = ctx.enter_context(tc.tile_pool(name="code", bufs=3))
        outs = ctx.enter_context(tc.tile_pool(name="outs", bufs=OUT_BUFS))
        ps_t = ctx.enter_context(tc.psum_pool(name="ps_t", bufs=4))
        ps_m = ctx.enter_context(tc.psum_pool(name="ps_m", bufs=4))

        vec = keep.tile([P, P], BF16, name="vec")
        nc.vector.memset(vec[:], 0.0)
        one = keep.tile([P, 1], F32, name="one")
        nc.vector.memset(one[:], 1.0)
        warm = keep.tile([P, 1], F32, name="warm")
        nc.scalar.sqrt(out=warm[:], in_=one[:])

        g_sb = []
        y_sb = []
        w_sb = keep.tile([P, PACK, IN_F], BF16, name="w_sb")
        for c, (j0, nj) in enumerate(CHUNKS):
            gt = keep.tile([P, nj, OUT_F], BF16, name="g%d" % c)
            yt = keep.tile([P, nj, OUT_F], BF16, name="y%d" % c)
            nc.sync.dma_start(out=gt[:], in_=g_v[:, j0 : j0 + nj, :])
            nc.sync.dma_start(out=yt[:], in_=y_v[:, j0 : j0 + nj, :])
            g_sb.append(gt)
            y_sb.append(yt)
            if c == 0:
                nc.sync.dma_start(out=vec[0:4, :], in_=running_var.rearrange("(t p) -> t p", p=P))
                nc.sync.dma_start(out=vec[4:8, :], in_=norm_weight.rearrange("(t p) -> t p", p=P))
                nc.sync.dma_start(out=w_sb[:], in_=w_v)

        ident_b = keep.tile([P, P], BF16, name="ident_b")
        make_identity(nc, ident_b[:])
        ident = keep.tile([P, P], F32, name="ident")
        make_identity(nc, ident[:])

        def where(g):
            j = g * GT
            for c, (j0, nj) in enumerate(CHUNKS):
                if j0 <= j < j0 + nj:
                    return g_sb[c], y_sb[c], j - j0
            raise ValueError("no chunk")

        prods = {}
        banks = {}
        grouped = {}
        words = {}

        def product(g, i):
            if not 0 <= g < NG or (g, i) in prods:
                return
            gt, yt, j = where(g)
            if i is None:
                pt = prod.tile([P, GT, OUT_F], F32, name="pt")
                nc.vector.tensor_tensor(out=pt[:], in0=gt[:, j : j + GT, :], in1=yt[:, j : j + GT, :], op=MULT)
                prods[(g, None)] = pt
                prods[(g, 0)] = pt[:, 0, :]
                prods[(g, 1)] = pt[:, 1, :]
                return
            pt = prod.tile([P, OUT_F], F32, name="pt%d" % i)
            eng = nc.gpsimd if i == 1 else nc.vector
            eng.tensor_tensor(out=pt[:], in0=gt[:, j + i, :], in1=yt[:, j + i, :], op=MULT)
            prods[(g, i)] = pt[:]

        def products(g):
            if G_SPLIT:
                for ahead in range(g + G_LEAD + 1):
                    product(ahead, 1)
                product(g, 0)
            else:
                product(g, None)

        def flip(g):
            got = []
            for i in range(GT):
                pt = prods[(g, i)]
                tp = ps_t.tile([P, PACK, P], F32, name="tp")
                for t in range(PACK):
                    nc.tensor.transpose(tp[:, t, :], pt[:, t * P : (t + 1) * P], ident[:])
                got.append(tp)
            banks[g] = got

        def scale(g):
            gr = grps.tile([P, GT, P, PACK], BF16, name="gr", align_bytes=64)
            for i in range(GT):
                nc.vector.tensor_tensor(
                    out=gr[:, i, :, :],
                    in0=banks[g][i][:].rearrange("p t m -> p m t"),
                    in1=c_bc,
                    op=MULT,
                )
            grouped[g] = gr

        def quantise(g):
            gr = grouped[g]
            cd = code.tile([P, GT * P], U32, name="cd", align_bytes=64)
            sc = code.tile([P, GT * P], U8, name="sc", align_bytes=64)
            for i in range(GT):
                nc.vector.quantize_mx(
                    out=cd[:, i * P : (i + 1) * P].bitcast(E5),
                    scales=sc[:, i * P : (i + 1) * P],
                    in_=gr[:, i, :, :].rearrange("p m t -> p (m t)"),
                )
            words[g] = (cd, sc)

        def multiply_store(g):
            cd, sc = words[g]
            first, count = store_of[g]
            if g == first:
                held[first] = outs.tile([P, count * GT, IN_F], F32, name="ot%d" % count)
            ot = held[first]
            for h in range(2):
                for i in range(GT):
                    acc = ps_m.tile([P, NH], F32, name="acc")
                    nc.tensor.matmul_mx(
                        out=acc[:],
                        lhsT=cd[:, i * P : (i + 1) * P].bitcast(E5),
                        lhsT_scale=sc[:, i * P : (i + 1) * P],
                        rhs=w_cd[h][:].bitcast(E4),
                        rhs_scale=w_sc[h][:],
                        start=True,
                        stop=True,
                    )
                    nc.scalar.copy(out=ot[:, (g - first) * GT + i, h * NH : (h + 1) * NH], in_=acc[:])
            if g == first + count - 1:
                nc.sync.dma_start(out=o_v[:, first * GT : (first + count) * GT, :], in_=ot[:])

        store_of = {}
        held = {}
        first_group = 0
        for count in STORES:
            for g in range(first_group, first_group + count):
                store_of[g] = (first_group, count)
            first_group += count
        assert first_group == NG

        products(0)

        vT = ps_t.tile([P, P], BF16, name="vT", tag="tp")
        nc.tensor.transpose(vT[:], vec[:], ident_b[:])
        var = keep.tile([P, PACK], F32, name="var")
        nc.vector.tensor_scalar_add(out=var[:], in0=vT[:, 0:PACK], scalar1=EPS)
        sd = keep.tile([P, PACK], F32, name="sd")
        nc.scalar.sqrt(out=sd[:], in_=var[:])
        flip(0)
        r0 = keep.tile([P, PACK], F32, name="r0")
        nc.vector.reciprocal(out=r0[:], in_=sd[:])
        hn = keep.tile([P, PACK], F32, name="hn")
        nc.vector.scalar_tensor_tensor(out=hn[:], in0=r0[:], scalar=-0.5, in1=r0[:], op0=MULT, op1=MULT)
        rn = keep.tile([P, PACK], F32, name="rn")
        nc.vector.tensor_tensor(out=rn[:], in0=vT[:, PACK : 2 * PACK], in1=r0[:], op=MULT)
        ev = keep.tile([P, PACK], F32, name="ev")
        nc.vector.tensor_tensor(out=ev[:], in0=hn[:], in1=var[:], op=MULT)
        c_sb = keep.tile([P, PACK], F32, name="c_sb")
        nc.vector.scalar_tensor_tensor(out=c_sb[:], in0=ev[:], scalar=1.5, in1=rn[:], op0=ADD, op1=MULT)
        c_bc = c_sb[:].unsqueeze(1).to_broadcast([P, P, PACK])

        scale(0)

        w_gr = []
        w_cd = []
        w_sc = []
        for h in range(2):
            wg = keep.tile([P, NH, PACK], BF16, name="wg%d" % h, align_bytes=64)
            src = w_sb[:, :, h * NH : (h + 1) * NH].rearrange("p t (c i) -> p c t i", i=4)
            dst = wg[:].rearrange("p (c i) t -> p c t i", i=4)
            if h == 0:
                nc.vector.tensor_copy(out=dst, in_=src)
            else:
                nc.scalar.copy(out=dst, in_=src)
            w_gr.append(wg)
            w_cd.append(keep.tile([P, NH], U32, name="wc%d" % h, align_bytes=64))
            w_sc.append(keep.tile([P, NH], U8, name="ws%d" % h, align_bytes=64))

        def quantise_weight(h):
            nc.vector.quantize_mx(
                out=w_cd[h][:].bitcast(E4),
                scales=w_sc[h][:],
                in_=w_gr[h][:].rearrange("p n t -> p (n t)"),
            )

        quantise(0)
        quantise_weight(0)
        quantise_weight(1)
        products(1)

        for g in range(NG):
            if g == 0:
                multiply_store(g)
                flip(g + 1)
                products(g + 2)
            else:
                if g + 1 < NG:
                    flip(g + 1)
                products(g + 2)
                multiply_store(g)
            if g + 1 < NG:
                scale(g + 1)
                quantise(g + 1)
